import numpy as np
import ml_dtypes


def mxq(x, axis, fmt="e4m3"):
    dtype, down = {"e4m3": (ml_dtypes.float8_e4m3fn, 7), "e5m2": (ml_dtypes.float8_e5m2, 14)}[fmt]
    v = np.moveaxis(np.asarray(x, np.float32).astype(ml_dtypes.bfloat16).astype(np.float64), axis, -1)
    blocks = v.reshape(v.shape[:-1] + (-1, 32))
    amax = np.abs(blocks).max(-1, keepdims=True)
    byte = np.maximum(np.where(amax > 0, np.frexp(amax)[1] - 1 + 127, 0) - down, 1)
    scale = np.exp2(byte - 127.0)
    codes = (blocks / scale).astype(np.float32).astype(dtype).astype(np.float64)
    return np.moveaxis((codes * scale).reshape(v.shape), -1, axis)


WIDE = False


def mx_kscale(k):
    if not WIDE:
        return np.ones(k)
    levels = np.array([10, -10, 5, -5, 0])
    a = np.random.permutation(np.resize(levels, k // 512 * 4)).reshape(k // 512, 4)
    idx = np.arange(k)
    return np.exp2(a[idx // 512, idx % 128 // 32])


BF16 = ml_dtypes.bfloat16


def bf(x):
    return np.asarray(x, np.float32).astype(BF16)


def f64(x):
    return np.asarray(x).astype(np.float64)


B, H, W, C, I, O, NH = 1, 2, 512, 512, 512, 512, 8
DH = I // NH
SCALE = DH ** -0.5


def setup_inputs():
    s, t = mx_kscale(C), mx_kscale(I)
    sc = s[None, :, None, None]
    return {"left_feat": bf(np.random.standard_normal((B, C, H, W)) * sc),
            "right_feat": bf(np.random.standard_normal((B, C, H, W)) * sc),
            "wq": bf(np.random.standard_normal((I, C)) / np.sqrt(C) / s[None, :] * t[:, None]),
            "wk": bf(np.random.standard_normal((I, C)) / np.sqrt(C) / s[None, :] / t[:, None])}


def reference(left_feat, right_feat, wq, wk):
    lf = f64(left_feat).reshape(B, C, H * W)
    rf = f64(right_feat).reshape(B, C, H * W)
    q = mxq(f64(wq), 1, "e4m3") @ mxq(lf, 1, "e4m3")
    k = mxq(f64(wk), 1, "e4m3") @ mxq(rf, 1, "e4m3")
    q = q.reshape(B, I, H, W).transpose(0, 2, 3, 1)
    k = k.reshape(B, I, H, W).transpose(0, 2, 1, 3)
    return (mxq(q, 3, "e4m3") @ mxq(k, 2, "e4m3")) * SCALE

@@ -1,0 +1,147 @@
+from contextlib import ExitStack
+
+import concourse.mybir as mybir
+from concourse.masks import make_identity
+
+F32 = mybir.dt.float32
+BF16 = mybir.dt.bfloat16
+U32 = mybir.dt.uint32
+U8 = mybir.dt.uint8
+FP8X4 = mybir.dt.float8_e4m3fn_x4
+
+P = 128
+PACK = 4
+K = P * PACK
+H = 2
+W = 512
+W_TILES = W // P
+SCALE = 0.125
+
+FLOPS = 2 * (2 * K * K * H * W) + 2 * H * W * W * K
+
+
+def quantise(nc, keep, grouped, name):
+    columns = grouped.shape[1]
+    codes = keep.tile([P, columns], U32, name=name + "_codes", align_bytes=64)
+    scales = keep.tile([P, columns], U8, name=name + "_scales", align_bytes=64)
+    nc.vector.quantize_mx(
+        out=codes[:].bitcast(FP8X4),
+        scales=scales[:],
+        in_=grouped.rearrange("p n j -> p (n j)"),
+    )
+    return codes, scales
+
+
+def load_weight(nc, keep, w, name):
+    rows = keep.tile([P, PACK, K], BF16, name=name + "_rows")
+    nc.sync.dma_start(out=rows[:], in_=w.rearrange("(p t) c -> p t c", t=PACK))
+    return rows
+
+
+def load_map(nc, keep, feat, h, name):
+    raw = keep.tile([P, PACK, W], BF16, name=name + "_raw")
+    nc.sync.dma_start(out=raw[:], in_=feat[0, :, h, :].rearrange("(p j) w -> p j w", j=PACK))
+    return raw
+
+
+def transpose_weight(nc, keep, psum_w, ident, rows, name):
+    words = rows[:].bitcast(F32).rearrange("p t (q u) -> p t u q", u=2)
+    grouped = keep.tile([P, PACK * P, PACK], BF16, name=name + "_grouped", align_bytes=64)
+    grouped_words = grouped[:].bitcast(F32).rearrange("p (t m) u -> p t m u", t=PACK)
+    for pair in range(PACK // 2):
+        bank = psum_w.tile([P, 2, 2, P], F32, name="w_bank")
+        for s in range(2):
+            for u in range(2):
+                nc.tensor.transpose(bank[:, s, u, :], words[:, 2 * pair + s, u, :], ident[:])
+        nc.scalar.copy(
+            out=grouped_words[:, 2 * pair : 2 * pair + 2, :, :],
+            in_=bank[:].rearrange("p s u m -> p s m u"),
+        )
+    return grouped
+
+
+def group_map(nc, keep, raw, name):
+    grouped = keep.tile([P, W, PACK], BF16, name=name + "_grouped", align_bytes=64)
+    nc.vector.tensor_copy(
+        out=grouped[:].rearrange("p (c i) j -> p c j i", i=4),
+        in_=raw[:].rearrange("p j (c i) -> p c j i", i=4),
+    )
+    return grouped
+
+
+def project(nc, keep, psum_p, weight, feat, name):
+    w_codes, w_scales = weight
+    x_codes, x_scales = feat
+    grouped = keep.tile([P, W, PACK], BF16, name=name + "_grouped", align_bytes=64)
+    for b in range(W_TILES):
+        cols = slice(b * P, (b + 1) * P)
+        bank = psum_p.tile([P, PACK, P], F32, name="p_bank")
+        for t in range(PACK):
+            o_cols = slice(t * P, (t + 1) * P)
+            nc.tensor.matmul_mx(
+                out=bank[:, t, :],
+                lhsT=w_codes[:, o_cols].bitcast(FP8X4),
+                lhsT_scale=w_scales[:, o_cols],
+                rhs=x_codes[:, cols].bitcast(FP8X4),
+                rhs_scale=x_scales[:, cols],
+                start=True,
+                stop=True,
+            )
+        nc.scalar.copy(out=grouped[:, cols, :], in_=bank[:].rearrange("p t n -> p n t"))
+    return grouped
+
+
+def scores(nc, keep, psum_d, q, k, out_h, name):
+    q_codes, q_scales = q
+    k_codes, k_scales = k
+    for b in range(W_TILES):
+        rows = slice(b * P, (b + 1) * P)
+        bank = psum_d.tile([P, W], F32, name="d_bank")
+        nc.tensor.matmul_mx(
+            out=bank[:],
+            lhsT=q_codes[:, rows].bitcast(FP8X4),
+            lhsT_scale=q_scales[:, rows],
+            rhs=k_codes[:].bitcast(FP8X4),
+            rhs_scale=k_scales[:],
+            start=True,
+            stop=True,
+        )
+        result = keep.tile([P, W], F32, name="%s_result%d" % (name, b))
+        if b % 2 == 0:
+            nc.scalar.mul(result[:], bank[:], SCALE)
+        else:
+            nc.vector.tensor_scalar_mul(result[:], bank[:], SCALE)
+        nc.sync.dma_start(out=out_h[rows, :], in_=result[:])
+
+
+def tile_sttm_single_pa_kernel(tc, left_feat, right_feat, wq, wk, out):
+    nc = tc.nc
+    with ExitStack() as ctx:
+        keep = ctx.enter_context(tc.tile_pool(name="keep", bufs=1))
+        psum_w = ctx.enter_context(tc.psum_pool(name="psum_w", bufs=2))
+        psum_p = ctx.enter_context(tc.psum_pool(name="psum_p", bufs=4))
+        psum_d = ctx.enter_context(tc.psum_pool(name="psum_d", bufs=2))
+
+        wk_rows = load_weight(nc, keep, wk, "wk")
+        r_raw = [load_map(nc, keep, right_feat, 0, "r0")]
+        wq_rows = load_weight(nc, keep, wq, "wq")
+        l_raw = [load_map(nc, keep, left_feat, 0, "l0")]
+        r_raw.append(load_map(nc, keep, right_feat, 1, "r1"))
+        l_raw.append(load_map(nc, keep, left_feat, 1, "l1"))
+
+        ident = keep.tile([P, P], F32, name="ident")
+        make_identity(nc, ident[:])
+
+        wk_grouped = transpose_weight(nc, keep, psum_w, ident, wk_rows, "wk")
+        wq_grouped = transpose_weight(nc, keep, psum_w, ident, wq_rows, "wq")
+        wk_mx = quantise(nc, keep, wk_grouped[:], "wk")
+        wq_mx = quantise(nc, keep, wq_grouped[:], "wq")
+
+        for h in range(H):
+            r_mx = quantise(nc, keep, group_map(nc, keep, r_raw[h], "r%d" % h)[:], "r%d" % h)
+            l_mx = quantise(nc, keep, group_map(nc, keep, l_raw[h], "l%d" % h)[:], "l%d" % h)
+            k_grouped = project(nc, keep, psum_p, wk_mx, r_mx, "k%d" % h)
+            q_grouped = project(nc, keep, psum_p, wq_mx, l_mx, "q%d" % h)
+            k_mx = quantise(nc, keep, k_grouped[:], "k%d" % h)
+            q_mx = quantise(nc, keep, q_grouped[:], "q%d" % h)
+            scores(nc, keep, psum_d, q_mx, k_mx, out[0, h], "d%d" % h)

@@ -20,16 +20,19 @@ SCALE = 0.125
 FLOPS = 2 * (2 * K * K * H * W) + 2 * H * W * W * K
 
 
-def quantise(nc, keep, grouped, name):
-    columns = grouped.shape[1]
+def mx_tiles(keep, columns, name):
     codes = keep.tile([P, columns], U32, name=name + "_codes", align_bytes=64)
     scales = keep.tile([P, columns], U8, name=name + "_scales", align_bytes=64)
-    nc.vector.quantize_mx(
-        out=codes[:].bitcast(FP8X4),
-        scales=scales[:],
-        in_=grouped.rearrange("p n j -> p (n j)"),
-    )
     return codes, scales
+
+
+def quantise(nc, grouped, mx, cols):
+    codes, scales = mx
+    nc.vector.quantize_mx(
+        out=codes[:, cols].bitcast(FP8X4),
+        scales=scales[:, cols],
+        in_=grouped[:, cols, :].rearrange("p n j -> p (n j)"),
+    )
 
 
 def load_weight(nc, keep, w, name):
@@ -44,12 +47,12 @@ def load_map(nc, keep, feat, h, name):
     return raw
 
 
-def transpose_weight(nc, keep, psum_w, ident, rows, name):
+def transpose_weight(nc, keep, psum_wd, ident, rows, name):
     words = rows[:].bitcast(F32).rearrange("p t (q u) -> p t u q", u=2)
-    grouped = keep.tile([P, PACK * P, PACK], BF16, name=name + "_grouped", align_bytes=64)
+    grouped = keep.tile([P, K, PACK], BF16, name=name + "_grouped", align_bytes=64)
     grouped_words = grouped[:].bitcast(F32).rearrange("p (t m) u -> p t m u", t=PACK)
     for pair in range(PACK // 2):
-        bank = psum_w.tile([P, 2, 2, P], F32, name="w_bank")
+        bank = psum_wd.tile([P, 2, 2, P], F32, name="w_bank", tag="wd")
         for s in range(2):
             for u in range(2):
                 nc.tensor.transpose(bank[:, s, u, :], words[:, 2 * pair + s, u, :], ident[:])
@@ -69,34 +72,34 @@ def group_map(nc, keep, raw, name):
     return grouped
 
 
-def project(nc, keep, psum_p, weight, feat, name):
+def project_block(nc, psum_p, weight, feat, grouped, b, on_vector):
     w_codes, w_scales = weight
     x_codes, x_scales = feat
-    grouped = keep.tile([P, W, PACK], BF16, name=name + "_grouped", align_bytes=64)
-    for b in range(W_TILES):
-        cols = slice(b * P, (b + 1) * P)
-        bank = psum_p.tile([P, PACK, P], F32, name="p_bank")
-        for t in range(PACK):
-            o_cols = slice(t * P, (t + 1) * P)
-            nc.tensor.matmul_mx(
-                out=bank[:, t, :],
-                lhsT=w_codes[:, o_cols].bitcast(FP8X4),
-                lhsT_scale=w_scales[:, o_cols],
-                rhs=x_codes[:, cols].bitcast(FP8X4),
-                rhs_scale=x_scales[:, cols],
-                start=True,
-                stop=True,
-            )
+    cols = slice(b * P, (b + 1) * P)
+    bank = psum_p.tile([P, PACK, P], F32, name="p_bank")
+    for t in range(PACK):
+        o_cols = slice(t * P, (t + 1) * P)
+        nc.tensor.matmul_mx(
+            out=bank[:, t, :],
+            lhsT=w_codes[:, o_cols].bitcast(FP8X4),
+            lhsT_scale=w_scales[:, o_cols],
+            rhs=x_codes[:, cols].bitcast(FP8X4),
+            rhs_scale=x_scales[:, cols],
+            start=True,
+            stop=True,
+        )
+    if on_vector:
+        nc.vector.tensor_copy(out=grouped[:, cols, :], in_=bank[:].rearrange("p t n -> p n t"))
+    else:
         nc.scalar.copy(out=grouped[:, cols, :], in_=bank[:].rearrange("p t n -> p n t"))
-    return grouped
 
 
-def scores(nc, keep, psum_d, q, k, out_h, name):
+def scores(nc, keep, psum_wd, q, k, out_h, name):
     q_codes, q_scales = q
     k_codes, k_scales = k
     for b in range(W_TILES):
         rows = slice(b * P, (b + 1) * P)
-        bank = psum_d.tile([P, W], F32, name="d_bank")
+        bank = psum_wd.tile([P, W], F32, name="d_bank", tag="wd")
         nc.tensor.matmul_mx(
             out=bank[:],
             lhsT=q_codes[:, rows].bitcast(FP8X4),
@@ -116,32 +119,58 @@ def scores(nc, keep, psum_d, q, k, out_h, name):
 
 def tile_sttm_single_pa_kernel(tc, left_feat, right_feat, wq, wk, out):
     nc = tc.nc
+    whole = slice(0, W)
     with ExitStack() as ctx:
         keep = ctx.enter_context(tc.tile_pool(name="keep", bufs=1))
-        psum_w = ctx.enter_context(tc.psum_pool(name="psum_w", bufs=2))
         psum_p = ctx.enter_context(tc.psum_pool(name="psum_p", bufs=4))
-        psum_d = ctx.enter_context(tc.psum_pool(name="psum_d", bufs=2))
+        psum_wd = ctx.enter_context(tc.psum_pool(name="psum_wd", bufs=4))
+        ctx.enter_context(tc.manual_schedule())
 
         wk_rows = load_weight(nc, keep, wk, "wk")
-        r_raw = [load_map(nc, keep, right_feat, 0, "r0")]
+        r0_raw = load_map(nc, keep, right_feat, 0, "r0")
         wq_rows = load_weight(nc, keep, wq, "wq")
-        l_raw = [load_map(nc, keep, left_feat, 0, "l0")]
-        r_raw.append(load_map(nc, keep, right_feat, 1, "r1"))
-        l_raw.append(load_map(nc, keep, left_feat, 1, "l1"))
+        l0_raw = load_map(nc, keep, left_feat, 0, "l0")
+        r1_raw = load_map(nc, keep, right_feat, 1, "r1")
+        l1_raw = load_map(nc, keep, left_feat, 1, "l1")
 
         ident = keep.tile([P, P], F32, name="ident")
         make_identity(nc, ident[:])
 
-        wk_grouped = transpose_weight(nc, keep, psum_w, ident, wk_rows, "wk")
-        wq_grouped = transpose_weight(nc, keep, psum_w, ident, wq_rows, "wq")
-        wk_mx = quantise(nc, keep, wk_grouped[:], "wk")
-        wq_mx = quantise(nc, keep, wq_grouped[:], "wq")
+        wk_mx = mx_tiles(keep, K, "wk")
+        wq_mx = mx_tiles(keep, K, "wq")
+        r_mx = [mx_tiles(keep, W, "r0"), mx_tiles(keep, W, "r1")]
+        l_mx = [mx_tiles(keep, W, "l0"), mx_tiles(keep, W, "l1")]
+        k_mx = [mx_tiles(keep, W, "k0"), mx_tiles(keep, W, "k1")]
+        q_mx = [mx_tiles(keep, W, "q0"), mx_tiles(keep, W, "q1")]
+        k_grouped = [keep.tile([P, W, PACK], BF16, name="k%d_grouped" % h, align_bytes=64) for h in range(H)]
+        q_grouped = [keep.tile([P, W, PACK], BF16, name="q%d_grouped" % h, align_bytes=64) for h in range(H)]
 
-        for h in range(H):
-            r_mx = quantise(nc, keep, group_map(nc, keep, r_raw[h], "r%d" % h)[:], "r%d" % h)
-            l_mx = quantise(nc, keep, group_map(nc, keep, l_raw[h], "l%d" % h)[:], "l%d" % h)
-            k_grouped = project(nc, keep, psum_p, wk_mx, r_mx, "k%d" % h)
-            q_grouped = project(nc, keep, psum_p, wq_mx, l_mx, "q%d" % h)
-            k_mx = quantise(nc, keep, k_grouped[:], "k%d" % h)
-            q_mx = quantise(nc, keep, q_grouped[:], "q%d" % h)
-            scores(nc, keep, psum_d, q_mx, k_mx, out[0, h], "d%d" % h)
+        wk_grouped = transpose_weight(nc, keep, psum_wd, ident, wk_rows, "wk")
+        r0_grouped = group_map(nc, keep, r0_raw, "r0")
+        quantise(nc, wk_grouped, wk_mx, whole)
+        quantise(nc, r0_grouped, r_mx[0], whole)
+        wq_grouped = transpose_weight(nc, keep, psum_wd, ident, wq_rows, "wq")
+        l0_grouped = group_map(nc, keep, l0_raw, "l0")
+        quantise(nc, wq_grouped, wq_mx, whole)
+        quantise(nc, l0_grouped, l_mx[0], whole)
+
+        for b in range(W_TILES):
+            project_block(nc, psum_p, wk_mx, r_mx[0], k_grouped[0], b, False)
+        r1_grouped = group_map(nc, keep, r1_raw, "r1")
+        quantise(nc, r1_grouped, r_mx[1], whole)
+        for b in range(W_TILES):
+            project_block(nc, psum_p, wq_mx, l_mx[0], q_grouped[0], b, False)
+        quantise(nc, k_grouped[0], k_mx[0], whole)
+        l1_grouped = group_map(nc, keep, l1_raw, "l1")
+        quantise(nc, q_grouped[0], q_mx[0], whole)
+        quantise(nc, l1_grouped, l_mx[1], whole)
+
+        for b in range(W_TILES):
+            project_block(nc, psum_p, wk_mx, r_mx[1], k_grouped[1], b, False)
+        scores(nc, keep, psum_wd, q_mx[0], k_mx[0], out[0, 0], "d0")
+        quantise(nc, k_grouped[1], k_mx[1], whole)
+        for pair in range(W_TILES // 2):
+            project_block(nc, psum_p, wq_mx, l_mx[1], q_grouped[1], 2 * pair, False)
+            project_block(nc, psum_p, wq_mx, l_mx[1], q_grouped[1], 2 * pair + 1, True)
+            quantise(nc, q_grouped[1], q_mx[1], slice(2 * pair * P, (2 * pair + 2) * P))
+        scores(nc, keep, psum_wd, q_mx[1], k_mx[1], out[0, 1], "d1")

@@ -15,6 +15,7 @@ K = P * PACK
 H = 2
 W = 512
 W_TILES = W // P
+HALF = W_TILES // 2
 SCALE = 0.125
 
 FLOPS = 2 * (2 * K * K * H * W) + 2 * H * W * W * K
@@ -72,7 +73,7 @@ def group_map(nc, keep, raw, name):
     return grouped
 
 
-def project_block(nc, psum_p, weight, feat, grouped, b, on_vector):
+def project_block(nc, psum_p, weight, feat, grouped, b):
     w_codes, w_scales = weight
     x_codes, x_scales = feat
     cols = slice(b * P, (b + 1) * P)
@@ -88,33 +89,33 @@ def project_block(nc, psum_p, weight, feat, grouped, b, on_vector):
             start=True,
             stop=True,
         )
-    if on_vector:
-        nc.vector.tensor_copy(out=grouped[:, cols, :], in_=bank[:].rearrange("p t n -> p n t"))
-    else:
-        nc.scalar.copy(out=grouped[:, cols, :], in_=bank[:].rearrange("p t n -> p n t"))
+    nc.scalar.copy(out=grouped[:, cols, :], in_=bank[:].rearrange("p t n -> p n t"))
 
 
-def scores(nc, keep, psum_wd, q, k, out_h, name):
+def score_pass(nc, psum_wd, q, k, b):
     q_codes, q_scales = q
     k_codes, k_scales = k
-    for b in range(W_TILES):
-        rows = slice(b * P, (b + 1) * P)
-        bank = psum_wd.tile([P, W], F32, name="d_bank", tag="wd")
-        nc.tensor.matmul_mx(
-            out=bank[:],
-            lhsT=q_codes[:, rows].bitcast(FP8X4),
-            lhsT_scale=q_scales[:, rows],
-            rhs=k_codes[:].bitcast(FP8X4),
-            rhs_scale=k_scales[:],
-            start=True,
-            stop=True,
-        )
-        result = keep.tile([P, W], F32, name="%s_result%d" % (name, b))
-        if b % 2 == 0:
-            nc.scalar.mul(result[:], bank[:], SCALE)
-        else:
-            nc.vector.tensor_scalar_mul(result[:], bank[:], SCALE)
-        nc.sync.dma_start(out=out_h[rows, :], in_=result[:])
+    rows = slice(b * P, (b + 1) * P)
+    bank = psum_wd.tile([P, W], F32, name="d_bank", tag="wd")
+    nc.tensor.matmul_mx(
+        out=bank[:],
+        lhsT=q_codes[:, rows].bitcast(FP8X4),
+        lhsT_scale=q_scales[:, rows],
+        rhs=k_codes[:].bitcast(FP8X4),
+        rhs_scale=k_scales[:],
+        start=True,
+        stop=True,
+    )
+    return bank
+
+
+def store_scores(nc, keep, bank, out_h, b, on_vector, name):
+    result = keep.tile([P, W], F32, name="%s_result%d" % (name, b))
+    if on_vector:
+        nc.vector.tensor_scalar_mul(result[:], bank[:], SCALE)
+    else:
+        nc.scalar.mul(result[:], bank[:], SCALE)
+    nc.sync.dma_start(out=out_h[b * P : (b + 1) * P, :], in_=result[:])
 
 
 def tile_sttm_single_pa_kernel(tc, left_feat, right_feat, wq, wk, out):
@@ -155,22 +156,29 @@ def tile_sttm_single_pa_kernel(tc, left_feat, right_feat, wq, wk, out):
         quantise(nc, l0_grouped, l_mx[0], whole)
 
         for b in range(W_TILES):
-            project_block(nc, psum_p, wk_mx, r_mx[0], k_grouped[0], b, False)
+            project_block(nc, psum_p, wk_mx, r_mx[0], k_grouped[0], b)
         r1_grouped = group_map(nc, keep, r1_raw, "r1")
-        quantise(nc, r1_grouped, r_mx[1], whole)
         for b in range(W_TILES):
-            project_block(nc, psum_p, wq_mx, l_mx[0], q_grouped[0], b, False)
+            project_block(nc, psum_p, wq_mx, l_mx[0], q_grouped[0], b)
         quantise(nc, k_grouped[0], k_mx[0], whole)
+        quantise(nc, r1_grouped, r_mx[1], whole)
         l1_grouped = group_map(nc, keep, l1_raw, "l1")
         quantise(nc, q_grouped[0], q_mx[0], whole)
         quantise(nc, l1_grouped, l_mx[1], whole)
 
         for b in range(W_TILES):
-            project_block(nc, psum_p, wk_mx, r_mx[1], k_grouped[1], b, False)
-        scores(nc, keep, psum_wd, q_mx[0], k_mx[0], out[0, 0], "d0")
+            project_block(nc, psum_p, wk_mx, r_mx[1], k_grouped[1], b)
+        d0_banks = [score_pass(nc, psum_wd, q_mx[0], k_mx[0], b) for b in range(W_TILES)]
+        for b in range(HALF):
+            store_scores(nc, keep, d0_banks[b], out[0, 0], b, True, "d0")
         quantise(nc, k_grouped[1], k_mx[1], whole)
-        for pair in range(W_TILES // 2):
-            project_block(nc, psum_p, wq_mx, l_mx[1], q_grouped[1], 2 * pair, False)
-            project_block(nc, psum_p, wq_mx, l_mx[1], q_grouped[1], 2 * pair + 1, True)
-            quantise(nc, q_grouped[1], q_mx[1], slice(2 * pair * P, (2 * pair + 2) * P))
-        scores(nc, keep, psum_wd, q_mx[1], k_mx[1], out[0, 1], "d1")
+        for b in range(W_TILES):
+            project_block(nc, psum_p, wq_mx, l_mx[1], q_grouped[1], b)
+        d1_banks = []
+        for b in range(W_TILES):
+            quantise(nc, q_grouped[1], q_mx[1], slice(b * P, (b + 1) * P))
+            d1_banks.append(score_pass(nc, psum_wd, q_mx[1], k_mx[1], b))
+            if b < HALF:
+                store_scores(nc, keep, d0_banks[HALF + b], out[0, 0], HALF + b, True, "d0")
+        for b in range(W_TILES):
+            store_scores(nc, keep, d1_banks[b], out[0, 1], b, b % 2 == 1, "d1")

@@ -163,7 +163,8 @@ def tile_sttm_single_pa_kernel(tc, left_feat, right_feat, wq, wk, out):
         quantise(nc, k_grouped[0], k_mx[0], whole)
         quantise(nc, r1_grouped, r_mx[1], whole)
         l1_grouped = group_map(nc, keep, l1_raw, "l1")
-        quantise(nc, q_grouped[0], q_mx[0], whole)
+        for b in range(W_TILES):
+            quantise(nc, q_grouped[0], q_mx[0], slice(b * P, (b + 1) * P))
         quantise(nc, l1_grouped, l_mx[1], whole)
 
         for b in range(W_TILES):

@@ -36,6 +36,12 @@ def quantise(nc, grouped, mx, cols):
     )
 
 
+def warm_up(nc, psum_p, zeros, count):
+    for i in range(count):
+        bank = psum_p.tile([P, W], F32, name="warm_bank", tag="p_bank")
+        nc.tensor.matmul(bank[:], lhsT=zeros[:, :P], rhs=zeros[:], start=True, stop=True)
+
+
 def load_weight(nc, keep, w, name):
     rows = keep.tile([P, PACK, K], BF16, name=name + "_rows")
     nc.sync.dma_start(out=rows[:], in_=w.rearrange("(p t) c -> p t c", t=PACK))
@@ -77,7 +83,7 @@ def project_block(nc, psum_p, weight, feat, grouped, b):
     w_codes, w_scales = weight
     x_codes, x_scales = feat
     cols = slice(b * P, (b + 1) * P)
-    bank = psum_p.tile([P, PACK, P], F32, name="p_bank")
+    bank = psum_p.tile([P, PACK, P], F32, name="p_bank", tag="p_bank")
     for t in range(PACK):
         o_cols = slice(t * P, (t + 1) * P)
         nc.tensor.matmul_mx(
@@ -134,6 +140,8 @@ def tile_sttm_single_pa_kernel(tc, left_feat, right_feat, wq, wk, out):
         r1_raw = load_map(nc, keep, right_feat, 1, "r1")
         l1_raw = load_map(nc, keep, left_feat, 1, "l1")
 
+        zeros = keep.tile([P, W], BF16, name="zeros")
+        nc.vector.memset(zeros[:], 0.0)
         ident = keep.tile([P, P], F32, name="ident")
         make_identity(nc, ident[:])
 
@@ -146,7 +154,9 @@ def tile_sttm_single_pa_kernel(tc, left_feat, right_feat, wq, wk, out):
         k_grouped = [keep.tile([P, W, PACK], BF16, name="k%d_grouped" % h, align_bytes=64) for h in range(H)]
         q_grouped = [keep.tile([P, W, PACK], BF16, name="q%d_grouped" % h, align_bytes=64) for h in range(H)]
 
+        warm_up(nc, psum_p, zeros, 5)
         wk_grouped = transpose_weight(nc, keep, psum_wd, ident, wk_rows, "wk")
+        warm_up(nc, psum_p, zeros, 2)
         r0_grouped = group_map(nc, keep, r0_raw, "r0")
         quantise(nc, wk_grouped, wk_mx, whole)
         quantise(nc, r0_grouped, r_mx[0], whole)

@@ -73,8 +73,8 @@ def transpose_weight(nc, keep, psum_wd, ident, rows, name):
 def group_map(nc, keep, raw, name):
     grouped = keep.tile([P, W, PACK], BF16, name=name + "_grouped", align_bytes=64)
     nc.vector.tensor_copy(
-        out=grouped[:].rearrange("p (c i) j -> p c j i", i=4),
-        in_=raw[:].rearrange("p j (c i) -> p c j i", i=4),
+        out=grouped[:].rearrange("p (c i) j -> p c j i", i=8),
+        in_=raw[:].rearrange("p j (c i) -> p c j i", i=8),
     )
     return grouped
 

@@ -156,7 +156,7 @@ def tile_sttm_single_pa_kernel(tc, left_feat, right_feat, wq, wk, out):
 
         warm_up(nc, psum_p, zeros, 5)
         wk_grouped = transpose_weight(nc, keep, psum_wd, ident, wk_rows, "wk")
-        warm_up(nc, psum_p, zeros, 2)
+        warm_up(nc, psum_p, zeros, 4)
         r0_grouped = group_map(nc, keep, r0_raw, "r0")
         quantise(nc, wk_grouped, wk_mx, whole)
         quantise(nc, r0_grouped, r_mx[0], whole)
@@ -173,18 +173,21 @@ def tile_sttm_single_pa_kernel(tc, left_feat, right_feat, wq, wk, out):
         quantise(nc, k_grouped[0], k_mx[0], whole)
         quantise(nc, r1_grouped, r_mx[1], whole)
         l1_grouped = group_map(nc, keep, l1_raw, "l1")
-        for b in range(W_TILES):
-            quantise(nc, q_grouped[0], q_mx[0], slice(b * P, (b + 1) * P))
+        quantise(nc, q_grouped[0], q_mx[0], slice(0, W // 2))
         quantise(nc, l1_grouped, l_mx[1], whole)
+        quantise(nc, q_grouped[0], q_mx[0], slice(W // 2, W))
 
         for b in range(W_TILES):
             project_block(nc, psum_p, wk_mx, r_mx[1], k_grouped[1], b)
-        d0_banks = [score_pass(nc, psum_wd, q_mx[0], k_mx[0], b) for b in range(W_TILES)]
+        d0_banks = []
+        for first in (0, HALF):
+            for b in range(first, first + HALF):
+                d0_banks.append(score_pass(nc, psum_wd, q_mx[0], k_mx[0], b))
+            for b in range(first, first + HALF):
+                project_block(nc, psum_p, wq_mx, l_mx[1], q_grouped[1], b)
         for b in range(HALF):
             store_scores(nc, keep, d0_banks[b], out[0, 0], b, True, "d0")
         quantise(nc, k_grouped[1], k_mx[1], whole)
-        for b in range(W_TILES):
-            project_block(nc, psum_p, wq_mx, l_mx[1], q_grouped[1], b)
         d1_banks = []
         for b in range(W_TILES):
             quantise(nc, q_grouped[1], q_mx[1], slice(b * P, (b + 1) * P))
@@ -192,4 +195,4 @@ def tile_sttm_single_pa_kernel(tc, left_feat, right_feat, wq, wk, out):
             if b < HALF:
                 store_scores(nc, keep, d0_banks[HALF + b], out[0, 0], HALF + b, True, "d0")
         for b in range(W_TILES):
-            store_scores(nc, keep, d1_banks[b], out[0, 1], b, b % 2 == 1, "d1")
+            store_scores(nc, keep, d1_banks[b], out[0, 1], b, b == W_TILES - 1, "d1")

from contextlib import ExitStack

import concourse.mybir as mybir
from concourse.masks import make_identity

F32 = mybir.dt.float32
BF16 = mybir.dt.bfloat16
U32 = mybir.dt.uint32
U8 = mybir.dt.uint8
FP8X4 = mybir.dt.float8_e4m3fn_x4

P = 128
PACK = 4
K = P * PACK
H = 2
W = 512
W_TILES = W // P
HALF = W_TILES // 2
SCALE = 0.125

FLOPS = 2 * (2 * K * K * H * W) + 2 * H * W * W * K


def mx_tiles(keep, columns, name):
    codes = keep.tile([P, columns], U32, name=name + "_codes", align_bytes=64)
    scales = keep.tile([P, columns], U8, name=name + "_scales", align_bytes=64)
    return codes, scales


def quantise(nc, grouped, mx, cols):
    codes, scales = mx
    nc.vector.quantize_mx(
        out=codes[:, cols].bitcast(FP8X4),
        scales=scales[:, cols],
        in_=grouped[:, cols, :].rearrange("p n j -> p (n j)"),
    )


def warm_up(nc, psum_p, zeros, count):
    for i in range(count):
        bank = psum_p.tile([P, W], F32, name="warm_bank", tag="p_bank")
        nc.tensor.matmul(bank[:], lhsT=zeros[:, :P], rhs=zeros[:], start=True, stop=True)


def load_weight(nc, keep, w, name):
    rows = keep.tile([P, PACK, K], BF16, name=name + "_rows")
    nc.sync.dma_start(out=rows[:], in_=w.rearrange("(p t) c -> p t c", t=PACK))
    return rows


def load_map(nc, keep, feat, h, name):
    raw = keep.tile([P, PACK, W], BF16, name=name + "_raw")
    nc.sync.dma_start(out=raw[:], in_=feat[0, :, h, :].rearrange("(p j) w -> p j w", j=PACK))
    return raw


def transpose_weight(nc, keep, psum_wd, ident, rows, name):
    words = rows[:].bitcast(F32).rearrange("p t (q u) -> p t u q", u=2)
    grouped = keep.tile([P, K, PACK], BF16, name=name + "_grouped", align_bytes=64)
    grouped_words = grouped[:].bitcast(F32).rearrange("p (t m) u -> p t m u", t=PACK)
    for pair in range(PACK // 2):
        bank = psum_wd.tile([P, 2, 2, P], F32, name="w_bank", tag="wd")
        for s in range(2):
            for u in range(2):
                nc.tensor.transpose(bank[:, s, u, :], words[:, 2 * pair + s, u, :], ident[:])
        nc.scalar.copy(
            out=grouped_words[:, 2 * pair : 2 * pair + 2, :, :],
            in_=bank[:].rearrange("p s u m -> p s m u"),
        )
    return grouped


def group_map(nc, keep, raw, name):
    grouped = keep.tile([P, W, PACK], BF16, name=name + "_grouped", align_bytes=64)
    nc.vector.tensor_copy(
        out=grouped[:].rearrange("p (c i) j -> p c j i", i=8),
        in_=raw[:].rearrange("p j (c i) -> p c j i", i=8),
    )
    return grouped


def project_block(nc, psum_p, weight, feat, grouped, b):
    w_codes, w_scales = weight
    x_codes, x_scales = feat
    cols = slice(b * P, (b + 1) * P)
    bank = psum_p.tile([P, PACK, P], F32, name="p_bank", tag="p_bank")
    for t in range(PACK):
        o_cols = slice(t * P, (t + 1) * P)
        nc.tensor.matmul_mx(
            out=bank[:, t, :],
            lhsT=w_codes[:, o_cols].bitcast(FP8X4),
            lhsT_scale=w_scales[:, o_cols],
            rhs=x_codes[:, cols].bitcast(FP8X4),
            rhs_scale=x_scales[:, cols],
            start=True,
            stop=True,
        )
    nc.scalar.copy(out=grouped[:, cols, :], in_=bank[:].rearrange("p t n -> p n t"))


def score_pass(nc, psum_wd, q, k, b):
    q_codes, q_scales = q
    k_codes, k_scales = k
    rows = slice(b * P, (b + 1) * P)
    bank = psum_wd.tile([P, W], F32, name="d_bank", tag="wd")
    nc.tensor.matmul_mx(
        out=bank[:],
        lhsT=q_codes[:, rows].bitcast(FP8X4),
        lhsT_scale=q_scales[:, rows],
        rhs=k_codes[:].bitcast(FP8X4),
        rhs_scale=k_scales[:],
        start=True,
        stop=True,
    )
    return bank


def store_scores(nc, keep, bank, out_h, b, on_vector, name):
    result = keep.tile([P, W], F32, name="%s_result%d" % (name, b))
    if on_vector:
        nc.vector.tensor_scalar_mul(result[:], bank[:], SCALE)
    else:
        nc.scalar.mul(result[:], bank[:], SCALE)
    nc.sync.dma_start(out=out_h[b * P : (b + 1) * P, :], in_=result[:])


def tile_sttm_single_pa_kernel(tc, left_feat, right_feat, wq, wk, out):
    nc = tc.nc
    whole = slice(0, W)
    with ExitStack() as ctx:
        keep = ctx.enter_context(tc.tile_pool(name="keep", bufs=1))
        psum_p = ctx.enter_context(tc.psum_pool(name="psum_p", bufs=4))
        psum_wd = ctx.enter_context(tc.psum_pool(name="psum_wd", bufs=4))
        ctx.enter_context(tc.manual_schedule())

        wk_rows = load_weight(nc, keep, wk, "wk")
        r0_raw = load_map(nc, keep, right_feat, 0, "r0")
        wq_rows = load_weight(nc, keep, wq, "wq")
        l0_raw = load_map(nc, keep, left_feat, 0, "l0")
        r1_raw = load_map(nc, keep, right_feat, 1, "r1")
        l1_raw = load_map(nc, keep, left_feat, 1, "l1")

        zeros = keep.tile([P, W], BF16, name="zeros")
        nc.vector.memset(zeros[:], 0.0)
        ident = keep.tile([P, P], F32, name="ident")
        make_identity(nc, ident[:])

        wk_mx = mx_tiles(keep, K, "wk")
        wq_mx = mx_tiles(keep, K, "wq")
        r_mx = [mx_tiles(keep, W, "r0"), mx_tiles(keep, W, "r1")]
        l_mx = [mx_tiles(keep, W, "l0"), mx_tiles(keep, W, "l1")]
        k_mx = [mx_tiles(keep, W, "k0"), mx_tiles(keep, W, "k1")]
        q_mx = [mx_tiles(keep, W, "q0"), mx_tiles(keep, W, "q1")]
        k_grouped = [keep.tile([P, W, PACK], BF16, name="k%d_grouped" % h, align_bytes=64) for h in range(H)]
        q_grouped = [keep.tile([P, W, PACK], BF16, name="q%d_grouped" % h, align_bytes=64) for h in range(H)]

        warm_up(nc, psum_p, zeros, 5)
        wk_grouped = transpose_weight(nc, keep, psum_wd, ident, wk_rows, "wk")
        warm_up(nc, psum_p, zeros, 4)
        r0_grouped = group_map(nc, keep, r0_raw, "r0")
        quantise(nc, wk_grouped, wk_mx, whole)
        quantise(nc, r0_grouped, r_mx[0], whole)
        wq_grouped = transpose_weight(nc, keep, psum_wd, ident, wq_rows, "wq")
        l0_grouped = group_map(nc, keep, l0_raw, "l0")
        quantise(nc, wq_grouped, wq_mx, whole)
        quantise(nc, l0_grouped, l_mx[0], whole)

        for b in range(W_TILES):
            project_block(nc, psum_p, wk_mx, r_mx[0], k_grouped[0], b)
        r1_grouped = group_map(nc, keep, r1_raw, "r1")
        for b in range(W_TILES):
            project_block(nc, psum_p, wq_mx, l_mx[0], q_grouped[0], b)
        quantise(nc, k_grouped[0], k_mx[0], whole)
        quantise(nc, r1_grouped, r_mx[1], whole)
        l1_grouped = group_map(nc, keep, l1_raw, "l1")
        quantise(nc, q_grouped[0], q_mx[0], slice(0, W // 2))
        quantise(nc, l1_grouped, l_mx[1], whole)
        quantise(nc, q_grouped[0], q_mx[0], slice(W // 2, W))

        for b in range(W_TILES):
            project_block(nc, psum_p, wk_mx, r_mx[1], k_grouped[1], b)
        d0_banks = []
        for first in (0, HALF):
            for b in range(first, first + HALF):
                d0_banks.append(score_pass(nc, psum_wd, q_mx[0], k_mx[0], b))
            for b in range(first, first + HALF):
                project_block(nc, psum_p, wq_mx, l_mx[1], q_grouped[1], b)
        for b in range(HALF):
            store_scores(nc, keep, d0_banks[b], out[0, 0], b, True, "d0")
        quantise(nc, k_grouped[1], k_mx[1], whole)
        d1_banks = []
        for b in range(W_TILES):
            quantise(nc, q_grouped[1], q_mx[1], slice(b * P, (b + 1) * P))
            d1_banks.append(score_pass(nc, psum_wd, q_mx[1], k_mx[1], b))
            if b < HALF:
                store_scores(nc, keep, d0_banks[HALF + b], out[0, 0], HALF + b, True, "d0")
        for b in range(W_TILES):
            store_scores(nc, keep, d1_banks[b], out[0, 1], b, b == W_TILES - 1, "d1")
